import numpy as np
import ml_dtypes


def mxq(x, axis, fmt="e4m3"):
    dtype, down = {"e4m3": (ml_dtypes.float8_e4m3fn, 7), "e5m2": (ml_dtypes.float8_e5m2, 14)}[fmt]
    v = np.moveaxis(np.asarray(x, np.float32).astype(ml_dtypes.bfloat16).astype(np.float64), axis, -1)
    blocks = v.reshape(v.shape[:-1] + (-1, 32))
    amax = np.abs(blocks).max(-1, keepdims=True)
    byte = np.maximum(np.where(amax > 0, np.frexp(amax)[1] - 1 + 127, 0) - down, 1)
    scale = np.exp2(byte - 127.0)
    codes = (blocks / scale).astype(np.float32).astype(dtype).astype(np.float64)
    return np.moveaxis((codes * scale).reshape(v.shape), -1, axis)


WIDE = False


def mx_kscale(k):
    if not WIDE:
        return np.ones(k)
    levels = np.array([10, -10, 5, -5, 0])
    if k % 512:
        return np.exp2(np.random.permutation(np.resize(levels, k // 32))).repeat(32)
    a = np.empty((k // 512, 16))
    for p in range(k // 512):
        a[p, :8] = np.random.permutation(np.resize(levels, 8))
        for g in range(8):
            far = levels[np.abs(levels - a[p, g]) >= 10]
            a[p, g + 8] = far[np.random.randint(len(far))]
    return np.exp2(a.ravel()).repeat(32)


BF16 = ml_dtypes.bfloat16


def bf(x):
    return np.asarray(x, np.float32).astype(BF16)


def f64(x):
    return np.asarray(x).astype(np.float64)


B, S, E, H = 2, 1024, 1024, 4
D = E // H
LN_EPS = 1e-6


def setup_inputs():
    s = mx_kscale(E)
    return {"h_attn": bf(np.random.standard_normal((B, H, S, D)) * 0.4 * s.reshape(H, 1, D)),
            "x": bf(np.random.standard_normal((B, S, E))),
            "out_w": bf(np.random.standard_normal((E, E)) * 2.0 / np.sqrt(E) / s[:, None]),
            "ln_gamma": bf(1.0 + 0.1 * np.random.standard_normal(E)),
            "ln_beta": bf(0.1 * np.random.standard_normal(E))}


def core(h_attn, x, out_w, ln_gamma, ln_beta):
    merged = f64(h_attn).transpose(0, 2, 1, 3).reshape(B, S, E)
    out = mxq(merged, 2, "e4m3") @ mxq(f64(out_w), 0, "e4m3")
    y = out + f64(x)
    mean = y.mean(-1, keepdims=True)
    var = np.square(y - mean).mean(-1, keepdims=True)
    return (y - mean) / np.sqrt(var + LN_EPS) * f64(ln_gamma) + f64(ln_beta)


def e4m3fn_bytes(y):
    return np.clip(np.asarray(y, np.float64), -448.0, 448.0).astype(np.float32).astype(ml_dtypes.float8_e4m3fn).view(np.uint8)


Y_SCALE = 210.0


def reference(h_attn, x, out_w, ln_gamma, ln_beta):
    out = core(h_attn, x, out_w, ln_gamma, ln_beta)
    return out, e4m3fn_bytes(out * Y_SCALE)

@@ -1,0 +1,310 @@
+from contextlib import ExitStack
+
+import concourse.masks as masks
+import concourse.mybir as mybir
+
+F32 = mybir.dt.float32
+BF16 = mybir.dt.bfloat16
+U32 = mybir.dt.uint32
+U8 = mybir.dt.uint8
+FP8X4 = mybir.dt.float8_e4m3fn_x4
+FP8 = mybir.dt.float8_e4m3fn
+ALU = mybir.AluOpType
+ACT = mybir.ActivationFunctionType
+
+B, H, S, D = 2, 4, 1024, 256
+E = H * D
+LN_EPS = 1e-6
+Y_SCALE = 210.0
+P = 128
+NT = B * S // P
+NH = 512
+FLOPS = 2 * B * S * E * E
+W_SPLIT = {(0, 0): 512, (1, 0): 256, (0, 1): 256, (1, 1): 256}
+CV = 256
+CV_TAIL = {NT - 3: 384, NT - 2: 768, NT - 1: E}
+PRELOAD = 12
+
+
+def tile_selfattention_pa_kernel(tc, h_attn, x, out_w, ln_gamma, ln_beta, out_0, out_1):
+    nc = tc.nc
+    xf = x.flatten_outer_dims()
+    o0 = out_0.flatten_outer_dims()
+    o1 = out_1.flatten_outer_dims()
+
+    with ExitStack() as ctx:
+        const = ctx.enter_context(tc.tile_pool(name="const", bufs=1))
+        inp = ctx.enter_context(tc.tile_pool(name="inp", bufs=NT))
+        st2 = ctx.enter_context(tc.tile_pool(name="st2", bufs=2))
+        st3 = ctx.enter_context(tc.tile_pool(name="st3", bufs=3))
+        st5 = ctx.enter_context(tc.tile_pool(name="st5", bufs=6))
+        ps_const = ctx.enter_context(tc.psum_pool(name="psconst", bufs=1))
+        ps_acc = ctx.enter_context(tc.psum_pool(name="psacc", bufs=2))
+        ps_tp = ctx.enter_context(tc.psum_pool(name="pstp", bufs=2))
+        ctx.enter_context(tc.manual_schedule())
+
+        hs, xs, tp, grp, mc, ms, acc = {}, {}, {}, {}, {}, {}, {}
+        y, sums, nmean, ssq, rstd, cen, res, res8 = {}, {}, {}, {}, {}, {}, {}, {}
+        wraw, wgrp, wc, ws = {}, {}, {}, {}
+
+        one_col = const.tile([P, 1], F32, name="one_col")
+        nc.vector.memset(one_col[:], 1.0)
+        warm = const.tile([P, 1], F32, name="warm")
+        nc.scalar.activation(out=warm[:], in_=one_col[:], func=ACT.Abs_reciprocal_sqrt)
+        gbrow = const.tile([P, 2 * E], BF16, name="gbrow")
+        nc.vector.memset(gbrow[:], 0.0)
+        ones = const.tile([P, P], BF16, name="ones")
+        nc.vector.memset(ones[:], 1.0)
+        ident = const.tile([P, P], F32, name="ident")
+        masks.make_identity(nc, ident[:])
+        nc.scalar.dma_start(out=gbrow[0:1, 0:E], in_=ln_gamma.rearrange("(o n) -> o n", o=1))
+        nc.scalar.dma_start(out=gbrow[0:1, E:2 * E], in_=ln_beta.rearrange("(o n) -> o n", o=1))
+        beta_sb = const.tile([P, E - CV], F32, name="beta_sb")
+
+        def load_h(j):
+            b, s0 = j // (S // P), (j % (S // P)) * P
+            t = inp.tile([P, H, D], BF16, name="hs", tag="hs")
+            nc.sync.dma_start(out=t[:], in_=h_attn[b, :, s0:s0 + P, :].rearrange("h s d -> s h d"))
+            hs[j] = t
+
+        def load_x(j):
+            t = inp.tile([P, E], BF16, name="xs", tag="xs")
+            nc.sync.dma_start(out=t[:], in_=xf[j * P:(j + 1) * P, :])
+            xs[j] = t
+
+        def load_w(g, nh, pieces):
+            t = const.tile([P, 4, NH], BF16, name="wraw%d%d" % (g, nh))
+            wide = NH // pieces
+            for c0 in range(0, NH, wide):
+                nc.sync.dma_start(
+                    out=t[:, :, c0:c0 + wide],
+                    in_=out_w[512 * g:512 * (g + 1), NH * nh + c0:NH * nh + c0 + wide].rearrange(
+                        "(p j) w -> p j w", j=4
+                    ),
+                )
+            wraw[(g, nh)] = t
+            wgrp[(g, nh)] = const.tile([P, NH, 4], BF16, name="wgrp%d%d" % (g, nh), align_bytes=64)
+
+        def w_copy_v(g, nh, c0, c1):
+            nc.vector.tensor_copy(
+                out=wgrp[(g, nh)][:, c0:c1, :].rearrange("p (c i) j -> p c j i", i=4),
+                in_=wraw[(g, nh)][:, :, c0:c1].rearrange("p j (c i) -> p c j i", i=4),
+            )
+
+        def w_copy_s(g, nh):
+            cut = W_SPLIT[(g, nh)]
+            nc.scalar.copy(
+                out=wgrp[(g, nh)][:, cut:NH, :].rearrange("p (c i) j -> p c j i", i=4),
+                in_=wraw[(g, nh)][:, :, cut:NH].rearrange("p j (c i) -> p c j i", i=4),
+            )
+
+        def w_quant(g, nh):
+            c = const.tile([P, NH], U32, name="wc%d%d" % (g, nh), align_bytes=64)
+            s = const.tile([P, NH], U8, name="ws%d%d" % (g, nh), align_bytes=64)
+            nc.vector.quantize_mx(
+                out=c[:].bitcast(FP8X4), scales=s[:], in_=wgrp[(g, nh)][:].rearrange("p w j -> p (w j)")
+            )
+            wc[(g, nh)] = c
+            ws[(g, nh)] = s
+
+        def transposes(j):
+            words = hs[j][:].rearrange("p h d -> p (h d)").bitcast(F32)
+            t = ps_tp.tile([P, 4, P], F32, name="tp", tag="tp")
+            for g in range(2):
+                for u in range(2):
+                    nc.tensor.transpose(t[:, 2 * g + u, :], words[:, 256 * g + u:256 * (g + 1):2], ident[:])
+            tp[j] = t
+
+        def copy_out(j):
+            t = st3.tile([P, 2 * P * 4], BF16, name="grp", tag="grp", align_bytes=64)
+            nc.scalar.copy(
+                out=t[:].bitcast(F32).rearrange("p (g r u) -> p g r u", g=2, u=2),
+                in_=tp[j][:].rearrange("p (g u) r -> p g r u", g=2),
+            )
+            grp[j] = t
+
+        def quant(j):
+            c = st3.tile([P, 2 * P], U32, name="mc", tag="mc", align_bytes=64)
+            s = st3.tile([P, 2 * P], U8, name="ms", tag="ms", align_bytes=64)
+            nc.vector.quantize_mx(out=c[:].bitcast(FP8X4), scales=s[:], in_=grp[j][:])
+            mc[j] = c
+            ms[j] = s
+
+        def matmuls(j, nh):
+            a = ps_acc.tile([P, NH], F32, name="acc%d" % nh, tag="acc%d" % nh)
+            for g in range(2):
+                nc.tensor.matmul_mx(
+                    out=a[:],
+                    lhsT=mc[j][:, P * g:P * (g + 1)].bitcast(FP8X4),
+                    lhsT_scale=ms[j][:, P * g:P * (g + 1)],
+                    rhs=wc[(g, nh)][:].bitcast(FP8X4),
+                    rhs_scale=ws[(g, nh)][:],
+                    start=(g == 0),
+                    stop=(g == 1),
+                )
+            acc[(j, nh)] = a
+
+        def add_x(j, nh):
+            if nh == 0:
+                y[j] = st3.tile([P, E], F32, name="y", tag="y")
+                sums[j] = st5.tile([P, 2], F32, name="sums", tag="sums")
+            cols = slice(NH * nh, NH * (nh + 1))
+            nc.vector.scalar_tensor_tensor(
+                out=y[j][:, cols], in0=acc[(j, nh)][:], scalar=1.0, in1=xs[j][:, cols],
+                op0=ALU.mult, op1=ALU.add, accum_out=sums[j][:, nh:nh + 1],
+            )
+
+        def stats(j):
+            scr = st5.tile([P, 2], F32, name="scr", tag="scr")
+            nmean[j] = st5.tile([P, 1], F32, name="nmean", tag="nmean")
+            nc.scalar.activation(out=scr[:], in_=sums[j][:], func=ACT.Copy, scale=-1.0 / E, accum_out=nmean[j][:])
+            junk = st2.tile([P, E], F32, name="junk", tag="junk")
+            ssq[j] = st5.tile([P, 1], F32, name="ssq", tag="ssq")
+            nc.scalar.activation(
+                out=junk[:], in_=y[j][:], func=ACT.Square, bias=nmean[j][:, 0:1], scale=1.0, accum_out=ssq[j][:],
+            )
+            rstd[j] = st5.tile([P, 1], F32, name="rstd", tag="rstd")
+            nc.scalar.activation(
+                out=rstd[j][:], in_=ssq[j][:], func=ACT.Abs_reciprocal_sqrt, bias=LN_EPS, scale=1.0 / E
+            )
+
+        def centre_gamma(j):
+            cen[j] = st3.tile([P, E], F32, name="cen", tag="cen")
+            nc.vector.scalar_tensor_tensor(
+                out=cen[j][:], in0=y[j][:], scalar=nmean[j][:, 0:1], in1=gam_ps[:], op0=ALU.add, op1=ALU.mult,
+            )
+            res[j] = st5.tile([P, E], F32, name="res", tag="res")
+            res8[j] = st5.tile([P, E], FP8, name="res8", tag="res8")
+
+        def scale_beta_v(j, c0, c1):
+            nc.vector.scalar_tensor_tensor(
+                out=res[j][:, c0:c1], in0=cen[j][:, c0:c1], scalar=rstd[j][:, 0:1], in1=bet_ps[:, c0:c1],
+                op0=ALU.mult, op1=ALU.add,
+            )
+
+        def scale_beta_g(j, c0):
+            w = st2.tile([P, E - CV], F32, name="w", tag="w")
+            nc.gpsimd.tensor_scalar(
+                out=w[:, c0 - CV:E - CV], in0=cen[j][:, c0:E], scalar1=rstd[j][:, 0:1], scalar2=0.0,
+                op0=ALU.mult, op1=ALU.add,
+            )
+            nc.gpsimd.tensor_tensor(
+                out=res[j][:, c0:E], in0=w[:, c0 - CV:E - CV], in1=beta_sb[:, c0 - CV:E - CV], op=ALU.add
+            )
+
+        def cast_s(j, c0, c1):
+            nc.scalar.activation(
+                out=res8[j][:, c0:c1], in_=res[j][:, c0:c1], func=ACT.Copy, scale=Y_SCALE, saturate=False
+            )
+
+        def cast_v(j, c0, c1):
+            nc.vector.tensor_scalar(
+                out=res8[j][:, c0:c1], in0=res[j][:, c0:c1], scalar1=Y_SCALE, scalar2=None, op0=ALU.mult,
+                saturate=False,
+            )
+
+        def store0(j, c0, c1):
+            nc.sync.dma_start(out=o0[j * P:(j + 1) * P, c0:c1], in_=res[j][:, c0:c1])
+
+        def store1(j, c0, c1):
+            nc.sync.dma_start(out=o1[j * P:(j + 1) * P, c0:c1], in_=res8[j][:, c0:c1].bitcast(U8))
+
+        load_w(0, 0, 2)
+        load_h(0)
+        load_w(1, 0, 1)
+        load_w(0, 1, 1)
+        load_w(1, 1, 1)
+        load_x(0)
+        load_h(1)
+        load_h(2)
+        for j in range(1, PRELOAD):
+            load_x(j)
+            if j + 2 < PRELOAD:
+                load_h(j + 2)
+
+        gam_ps = ps_const.tile([P, E], BF16, name="gam_ps")
+        bet_ps = ps_const.tile([P, E], BF16, name="bet_ps")
+
+        def spread(dst, c0):
+            for nh in range(2):
+                nc.tensor.matmul(out=dst[:, NH * nh:NH * (nh + 1)], lhsT=ones[:],
+                                 rhs=gbrow[:, c0 + NH * nh:c0 + NH * (nh + 1)], start=True, stop=True)
+
+        w_copy_v(0, 0, 0, NH // 2)
+        w_copy_v(0, 0, NH // 2, NH)
+        transposes(0)
+        spread(gam_ps, 0)
+        copy_out(0)
+        w_quant(0, 0)
+        w_copy_v(1, 0, 0, W_SPLIT[(1, 0)])
+        w_copy_s(1, 0)
+        quant(0)
+        w_copy_v(0, 1, 0, W_SPLIT[(0, 1)])
+        w_copy_s(0, 1)
+        w_quant(1, 0)
+        matmuls(0, 0)
+        transposes(1)
+        spread(bet_ps, E)
+        transposes(2)
+        w_copy_v(1, 1, 0, W_SPLIT[(1, 1)])
+        w_copy_s(1, 1)
+        w_quant(0, 1)
+        add_x(0, 0)
+        w_quant(1, 1)
+        matmuls(0, 1)
+        copy_out(1)
+        quant(1)
+        matmuls(1, 0)
+        matmuls(1, 1)
+        transposes(3)
+        copy_out(2)
+        quant(2)
+        nc.scalar.copy(out=beta_sb[:], in_=bet_ps[:, CV:E])
+        add_x(0, 1)
+        stats(0)
+        copy_out(3)
+
+        for i in range(NT):
+            if i + 2 < NT:
+                matmuls(i + 2, 0)
+            if i + 4 < NT:
+                transposes(i + 4)
+            if i + 2 < NT:
+                matmuls(i + 2, 1)
+            if i + 1 < NT:
+                add_x(i + 1, 0)
+                add_x(i + 1, 1)
+                stats(i + 1)
+            if 1 <= i < NT - 1:
+                scale_beta_v(i - 1, 0, CV_TAIL.get(i - 1, CV))
+            centre_gamma(i)
+            if i == NT - 1:
+                scale_beta_v(i - 1, 0, CV_TAIL.get(i - 1, CV))
+            if i + 3 < NT:
+                quant(i + 3)
+            if i < NT - 1:
+                scale_beta_g(i, CV_TAIL.get(i, CV))
+            if i + 4 < NT:
+                copy_out(i + 4)
+            if 1 <= i < NT - 1:
+                store0(i - 1, 0, E)
+                cast_s(i - 1, 0, E)
+                store1(i - 1, 0, E)
+                if i - 1 + PRELOAD < NT:
+                    load_h(i - 1 + PRELOAD)
+                    load_x(i - 1 + PRELOAD)
+
+        last = NT - 1
+        store0(last - 1, 0, E)
+        cast_s(last - 1, 0, NH)
+        store1(last - 1, 0, NH)
+        scale_beta_v(last, 0, NH)
+        store0(last, 0, NH)
+        cast_s(last, 0, NH)
+        store1(last, 0, NH)
+        cast_v(last - 1, NH, E)
+        store1(last - 1, NH, E)
+        scale_beta_v(last, NH, E)
+        store0(last, NH, E)
+        cast_v(last, NH, E)
+        store1(last, NH, E)

@@ -20,7 +20,7 @@ P = 128
 NT = B * S // P
 NH = 512
 FLOPS = 2 * B * S * E * E
-W_SPLIT = {(0, 0): 512, (1, 0): 256, (0, 1): 256, (1, 1): 256}
+W_SPLIT = {(0, 0): 512, (1, 0): 288, (0, 1): 256, (1, 1): 256}
 CV = 256
 CV_TAIL = {NT - 3: 384, NT - 2: 768, NT - 1: E}
 PRELOAD = 12
@@ -51,10 +51,10 @@ def tile_selfattention_pa_kernel(tc, h_attn, x, out_w, ln_gamma, ln_beta, out_0,
         nc.vector.memset(one_col[:], 1.0)
         warm = const.tile([P, 1], F32, name="warm")
         nc.scalar.activation(out=warm[:], in_=one_col[:], func=ACT.Abs_reciprocal_sqrt)
-        gbrow = const.tile([P, 2 * E], BF16, name="gbrow")
-        nc.vector.memset(gbrow[:], 0.0)
         ones = const.tile([P, P], BF16, name="ones")
         nc.vector.memset(ones[:], 1.0)
+        gbrow = const.tile([P, 2 * E], BF16, name="gbrow")
+        nc.vector.memset(gbrow[:], 0.0)
         ident = const.tile([P, P], F32, name="ident")
         masks.make_identity(nc, ident[:])
         nc.scalar.dma_start(out=gbrow[0:1, 0:E], in_=ln_gamma.rearrange("(o n) -> o n", o=1))
@@ -209,8 +209,8 @@ def tile_selfattention_pa_kernel(tc, h_attn, x, out_w, ln_gamma, ln_beta, out_0,
         def store1(j, c0, c1):
             nc.sync.dma_start(out=o1[j * P:(j + 1) * P, c0:c1], in_=res8[j][:, c0:c1].bitcast(U8))
 
-        load_w(0, 0, 2)
         load_h(0)
+        load_w(0, 0, 2)
         load_w(1, 0, 1)
         load_w(0, 1, 1)
         load_w(1, 1, 1)
@@ -230,39 +230,53 @@ def tile_selfattention_pa_kernel(tc, h_attn, x, out_w, ln_gamma, ln_beta, out_0,
                 nc.tensor.matmul(out=dst[:, NH * nh:NH * (nh + 1)], lhsT=ones[:],
                                  rhs=gbrow[:, c0 + NH * nh:c0 + NH * (nh + 1)], start=True, stop=True)
 
+        def keep_clock(rhs):
+            nc.tensor.matmul(out=bet_ps[:, 0:rhs.shape[1]], lhsT=ones[:], rhs=rhs, start=True, stop=True)
+
+        for rep in range(16):
+            keep_clock(ones[:])
+        transposes(0)
+        for c0 in (0, NH // 2):
+            for t in range(2):
+                keep_clock(wraw[(0, 0)][:, t, c0:c0 + NH // 2])
         w_copy_v(0, 0, 0, NH // 2)
         w_copy_v(0, 0, NH // 2, NH)
-        transposes(0)
-        spread(gam_ps, 0)
         copy_out(0)
         w_quant(0, 0)
+        for t in range(2):
+            keep_clock(wraw[(1, 0)][:, t, :])
         w_copy_v(1, 0, 0, W_SPLIT[(1, 0)])
         w_copy_s(1, 0)
         quant(0)
+        for t in range(2):
+            keep_clock(wraw[(0, 1)][:, t, :])
         w_copy_v(0, 1, 0, W_SPLIT[(0, 1)])
         w_copy_s(0, 1)
         w_quant(1, 0)
         matmuls(0, 0)
-        transposes(1)
-        spread(bet_ps, E)
-        transposes(2)
+        for t in range(2):
+            keep_clock(wraw[(1, 1)][:, t, :])
         w_copy_v(1, 1, 0, W_SPLIT[(1, 1)])
         w_copy_s(1, 1)
         w_quant(0, 1)
-        add_x(0, 0)
+        spread(gam_ps, 0)
+        transposes(1)
         w_quant(1, 1)
         matmuls(0, 1)
+        add_x(0, 0)
         copy_out(1)
         quant(1)
+        spread(bet_ps, E)
+        transposes(2)
         matmuls(1, 0)
         matmuls(1, 1)
-        transposes(3)
+        add_x(0, 1)
         copy_out(2)
         quant(2)
-        nc.scalar.copy(out=beta_sb[:], in_=bet_ps[:, CV:E])
-        add_x(0, 1)
         stats(0)
+        transposes(3)
         copy_out(3)
+        nc.scalar.copy(out=beta_sb[:], in_=bet_ps[:, CV:E])
 
         for i in range(NT):
             if i + 2 < NT:

@@ -21,7 +21,7 @@ NT = B * S // P
 NH = 512
 FLOPS = 2 * B * S * E * E
 W_SPLIT = {(0, 0): 512, (1, 0): 288, (0, 1): 256, (1, 1): 256}
-CV = 256
+CV = 320
 CV_TAIL = {NT - 3: 384, NT - 2: 768, NT - 1: E}
 PRELOAD = 12
 

@@ -21,7 +21,7 @@ NT = B * S // P
 NH = 512
 FLOPS = 2 * B * S * E * E
 W_SPLIT = {(0, 0): 512, (1, 0): 288, (0, 1): 256, (1, 1): 256}
-CV = 320
+CV = 336
 CV_TAIL = {NT - 3: 384, NT - 2: 768, NT - 1: E}
 PRELOAD = 12
 
@@ -154,10 +154,14 @@ def tile_selfattention_pa_kernel(tc, h_attn, x, out_w, ln_gamma, ln_beta, out_0,
                 op0=ALU.mult, op1=ALU.add, accum_out=sums[j][:, nh:nh + 1],
             )
 
-        def stats(j):
-            scr = st5.tile([P, 2], F32, name="scr", tag="scr")
+        def mean(j):
             nmean[j] = st5.tile([P, 1], F32, name="nmean", tag="nmean")
-            nc.scalar.activation(out=scr[:], in_=sums[j][:], func=ACT.Copy, scale=-1.0 / E, accum_out=nmean[j][:])
+            nc.vector.tensor_scalar(
+                out=nmean[j][:], in0=sums[j][:, 0:1], scalar1=sums[j][:, 1:2], scalar2=-1.0 / E,
+                op0=ALU.add, op1=ALU.mult,
+            )
+
+        def stats(j):
             junk = st2.tile([P, E], F32, name="junk", tag="junk")
             ssq[j] = st5.tile([P, 1], F32, name="ssq", tag="ssq")
             nc.scalar.activation(
@@ -260,23 +264,24 @@ def tile_selfattention_pa_kernel(tc, h_attn, x, out_w, ln_gamma, ln_beta, out_0,
         w_copy_s(1, 1)
         w_quant(0, 1)
         spread(gam_ps, 0)
+        spread(bet_ps, E)
         transposes(1)
         w_quant(1, 1)
         matmuls(0, 1)
         add_x(0, 0)
         copy_out(1)
         quant(1)
-        spread(bet_ps, E)
+        nc.scalar.copy(out=beta_sb[:], in_=bet_ps[:, CV:E])
         transposes(2)
         matmuls(1, 0)
         matmuls(1, 1)
         add_x(0, 1)
+        mean(0)
         copy_out(2)
         quant(2)
         stats(0)
         transposes(3)
         copy_out(3)
-        nc.scalar.copy(out=beta_sb[:], in_=bet_ps[:, CV:E])
 
         for i in range(NT):
             if i + 2 < NT:
@@ -288,9 +293,11 @@ def tile_selfattention_pa_kernel(tc, h_attn, x, out_w, ln_gamma, ln_beta, out_0,
             if i + 1 < NT:
                 add_x(i + 1, 0)
                 add_x(i + 1, 1)
-                stats(i + 1)
             if 1 <= i < NT - 1:
                 scale_beta_v(i - 1, 0, CV_TAIL.get(i - 1, CV))
+            if i + 1 < NT:
+                mean(i + 1)
+                stats(i + 1)
             centre_gamma(i)
             if i == NT - 1:
                 scale_beta_v(i - 1, 0, CV_TAIL.get(i - 1, CV))

@@ -20,7 +20,7 @@ P = 128
 NT = B * S // P
 NH = 512
 FLOPS = 2 * B * S * E * E
-W_SPLIT = {(0, 0): 512, (1, 0): 288, (0, 1): 256, (1, 1): 256}
+W_SPLIT = {(0, 0): 512, (1, 0): 368, (0, 1): 256, (1, 1): 256}
 CV = 336
 CV_TAIL = {NT - 3: 384, NT - 2: 768, NT - 1: E}
 PRELOAD = 12
@@ -215,11 +215,11 @@ def tile_selfattention_pa_kernel(tc, h_attn, x, out_w, ln_gamma, ln_beta, out_0,
 
         load_h(0)
         load_w(0, 0, 2)
+        load_h(1)
         load_w(1, 0, 1)
         load_w(0, 1, 1)
         load_w(1, 1, 1)
         load_x(0)
-        load_h(1)
         load_h(2)
         for j in range(1, PRELOAD):
             load_x(j)
@@ -247,17 +247,20 @@ def tile_selfattention_pa_kernel(tc, h_attn, x, out_w, ln_gamma, ln_beta, out_0,
         w_copy_v(0, 0, NH // 2, NH)
         copy_out(0)
         w_quant(0, 0)
+        transposes(1)
+        copy_out(1)
+        quant(0)
         for t in range(2):
             keep_clock(wraw[(1, 0)][:, t, :])
         w_copy_v(1, 0, 0, W_SPLIT[(1, 0)])
         w_copy_s(1, 0)
-        quant(0)
+        quant(1)
         for t in range(2):
             keep_clock(wraw[(0, 1)][:, t, :])
-        w_copy_v(0, 1, 0, W_SPLIT[(0, 1)])
-        w_copy_s(0, 1)
         w_quant(1, 0)
         matmuls(0, 0)
+        w_copy_v(0, 1, 0, W_SPLIT[(0, 1)])
+        w_copy_s(0, 1)
         for t in range(2):
             keep_clock(wraw[(1, 1)][:, t, :])
         w_copy_v(1, 1, 0, W_SPLIT[(1, 1)])
@@ -265,14 +268,11 @@ def tile_selfattention_pa_kernel(tc, h_attn, x, out_w, ln_gamma, ln_beta, out_0,
         w_quant(0, 1)
         spread(gam_ps, 0)
         spread(bet_ps, E)
-        transposes(1)
+        transposes(2)
         w_quant(1, 1)
         matmuls(0, 1)
         add_x(0, 0)
-        copy_out(1)
-        quant(1)
         nc.scalar.copy(out=beta_sb[:], in_=bet_ps[:, CV:E])
-        transposes(2)
         matmuls(1, 0)
         matmuls(1, 1)
         add_x(0, 1)

@@ -323,9 +323,9 @@ def tile_selfattention_pa_kernel(tc, h_attn, x, out_w, ln_gamma, ln_beta, out_0,
         store0(last, 0, NH)
         cast_s(last, 0, NH)
         store1(last, 0, NH)
-        cast_v(last - 1, NH, E)
-        store1(last - 1, NH, E)
         scale_beta_v(last, NH, E)
         store0(last, NH, E)
+        cast_v(last - 1, NH, E)
+        store1(last - 1, NH, E)
         cast_v(last, NH, E)
         store1(last, NH, E)

@@ -167,6 +167,8 @@ def tile_selfattention_pa_kernel(tc, h_attn, x, out_w, ln_gamma, ln_beta, out_0,
             nc.scalar.activation(
                 out=junk[:], in_=y[j][:], func=ACT.Square, bias=nmean[j][:, 0:1], scale=1.0, accum_out=ssq[j][:],
             )
+
+        def make_rstd(j):
             rstd[j] = st5.tile([P, 1], F32, name="rstd", tag="rstd")
             nc.scalar.activation(
                 out=rstd[j][:], in_=ssq[j][:], func=ACT.Abs_reciprocal_sqrt, bias=LN_EPS, scale=1.0 / E
@@ -280,6 +282,7 @@ def tile_selfattention_pa_kernel(tc, h_attn, x, out_w, ln_gamma, ln_beta, out_0,
         copy_out(2)
         quant(2)
         stats(0)
+        make_rstd(0)
         transposes(3)
         copy_out(3)
 
@@ -307,6 +310,8 @@ def tile_selfattention_pa_kernel(tc, h_attn, x, out_w, ln_gamma, ln_beta, out_0,
                 scale_beta_g(i, CV_TAIL.get(i, CV))
             if i + 4 < NT:
                 copy_out(i + 4)
+            if i + 1 < NT:
+                make_rstd(i + 1)
             if 1 <= i < NT - 1:
                 store0(i - 1, 0, E)
                 cast_s(i - 1, 0, E)

from contextlib import ExitStack

import concourse.masks as masks
import concourse.mybir as mybir

F32 = mybir.dt.float32
BF16 = mybir.dt.bfloat16
U32 = mybir.dt.uint32
U8 = mybir.dt.uint8
FP8X4 = mybir.dt.float8_e4m3fn_x4
FP8 = mybir.dt.float8_e4m3fn
ALU = mybir.AluOpType
ACT = mybir.ActivationFunctionType

B, H, S, D = 2, 4, 1024, 256
E = H * D
LN_EPS = 1e-6
Y_SCALE = 210.0
P = 128
NT = B * S // P
NH = 512
FLOPS = 2 * B * S * E * E
W_SPLIT = {(0, 0): 512, (1, 0): 368, (0, 1): 256, (1, 1): 256}
CV = 336
CV_TAIL = {NT - 3: 384, NT - 2: 768, NT - 1: E}
PRELOAD = 12


def tile_selfattention_pa_kernel(tc, h_attn, x, out_w, ln_gamma, ln_beta, out_0, out_1):
    nc = tc.nc
    xf = x.flatten_outer_dims()
    o0 = out_0.flatten_outer_dims()
    o1 = out_1.flatten_outer_dims()

    with ExitStack() as ctx:
        const = ctx.enter_context(tc.tile_pool(name="const", bufs=1))
        inp = ctx.enter_context(tc.tile_pool(name="inp", bufs=NT))
        st2 = ctx.enter_context(tc.tile_pool(name="st2", bufs=2))
        st3 = ctx.enter_context(tc.tile_pool(name="st3", bufs=3))
        st5 = ctx.enter_context(tc.tile_pool(name="st5", bufs=6))
        ps_const = ctx.enter_context(tc.psum_pool(name="psconst", bufs=1))
        ps_acc = ctx.enter_context(tc.psum_pool(name="psacc", bufs=2))
        ps_tp = ctx.enter_context(tc.psum_pool(name="pstp", bufs=2))
        ctx.enter_context(tc.manual_schedule())

        hs, xs, tp, grp, mc, ms, acc = {}, {}, {}, {}, {}, {}, {}
        y, sums, nmean, ssq, rstd, cen, res, res8 = {}, {}, {}, {}, {}, {}, {}, {}
        wraw, wgrp, wc, ws = {}, {}, {}, {}

        one_col = const.tile([P, 1], F32, name="one_col")
        nc.vector.memset(one_col[:], 1.0)
        warm = const.tile([P, 1], F32, name="warm")
        nc.scalar.activation(out=warm[:], in_=one_col[:], func=ACT.Abs_reciprocal_sqrt)
        ones = const.tile([P, P], BF16, name="ones")
        nc.vector.memset(ones[:], 1.0)
        gbrow = const.tile([P, 2 * E], BF16, name="gbrow")
        nc.vector.memset(gbrow[:], 0.0)
        ident = const.tile([P, P], F32, name="ident")
        masks.make_identity(nc, ident[:])
        nc.scalar.dma_start(out=gbrow[0:1, 0:E], in_=ln_gamma.rearrange("(o n) -> o n", o=1))
        nc.scalar.dma_start(out=gbrow[0:1, E:2 * E], in_=ln_beta.rearrange("(o n) -> o n", o=1))
        beta_sb = const.tile([P, E - CV], F32, name="beta_sb")

        def load_h(j):
            b, s0 = j // (S // P), (j % (S // P)) * P
            t = inp.tile([P, H, D], BF16, name="hs", tag="hs")
            nc.sync.dma_start(out=t[:], in_=h_attn[b, :, s0:s0 + P, :].rearrange("h s d -> s h d"))
            hs[j] = t

        def load_x(j):
            t = inp.tile([P, E], BF16, name="xs", tag="xs")
            nc.sync.dma_start(out=t[:], in_=xf[j * P:(j + 1) * P, :])
            xs[j] = t

        def load_w(g, nh, pieces):
            t = const.tile([P, 4, NH], BF16, name="wraw%d%d" % (g, nh))
            wide = NH // pieces
            for c0 in range(0, NH, wide):
                nc.sync.dma_start(
                    out=t[:, :, c0:c0 + wide],
                    in_=out_w[512 * g:512 * (g + 1), NH * nh + c0:NH * nh + c0 + wide].rearrange(
                        "(p j) w -> p j w", j=4
                    ),
                )
            wraw[(g, nh)] = t
            wgrp[(g, nh)] = const.tile([P, NH, 4], BF16, name="wgrp%d%d" % (g, nh), align_bytes=64)

        def w_copy_v(g, nh, c0, c1):
            nc.vector.tensor_copy(
                out=wgrp[(g, nh)][:, c0:c1, :].rearrange("p (c i) j -> p c j i", i=4),
                in_=wraw[(g, nh)][:, :, c0:c1].rearrange("p j (c i) -> p c j i", i=4),
            )

        def w_copy_s(g, nh):
            cut = W_SPLIT[(g, nh)]
            nc.scalar.copy(
                out=wgrp[(g, nh)][:, cut:NH, :].rearrange("p (c i) j -> p c j i", i=4),
                in_=wraw[(g, nh)][:, :, cut:NH].rearrange("p j (c i) -> p c j i", i=4),
            )

        def w_quant(g, nh):
            c = const.tile([P, NH], U32, name="wc%d%d" % (g, nh), align_bytes=64)
            s = const.tile([P, NH], U8, name="ws%d%d" % (g, nh), align_bytes=64)
            nc.vector.quantize_mx(
                out=c[:].bitcast(FP8X4), scales=s[:], in_=wgrp[(g, nh)][:].rearrange("p w j -> p (w j)")
            )
            wc[(g, nh)] = c
            ws[(g, nh)] = s

        def transposes(j):
            words = hs[j][:].rearrange("p h d -> p (h d)").bitcast(F32)
            t = ps_tp.tile([P, 4, P], F32, name="tp", tag="tp")
            for g in range(2):
                for u in range(2):
                    nc.tensor.transpose(t[:, 2 * g + u, :], words[:, 256 * g + u:256 * (g + 1):2], ident[:])
            tp[j] = t

        def copy_out(j):
            t = st3.tile([P, 2 * P * 4], BF16, name="grp", tag="grp", align_bytes=64)
            nc.scalar.copy(
                out=t[:].bitcast(F32).rearrange("p (g r u) -> p g r u", g=2, u=2),
                in_=tp[j][:].rearrange("p (g u) r -> p g r u", g=2),
            )
            grp[j] = t

        def quant(j):
            c = st3.tile([P, 2 * P], U32, name="mc", tag="mc", align_bytes=64)
            s = st3.tile([P, 2 * P], U8, name="ms", tag="ms", align_bytes=64)
            nc.vector.quantize_mx(out=c[:].bitcast(FP8X4), scales=s[:], in_=grp[j][:])
            mc[j] = c
            ms[j] = s

        def matmuls(j, nh):
            a = ps_acc.tile([P, NH], F32, name="acc%d" % nh, tag="acc%d" % nh)
            for g in range(2):
                nc.tensor.matmul_mx(
                    out=a[:],
                    lhsT=mc[j][:, P * g:P * (g + 1)].bitcast(FP8X4),
                    lhsT_scale=ms[j][:, P * g:P * (g + 1)],
                    rhs=wc[(g, nh)][:].bitcast(FP8X4),
                    rhs_scale=ws[(g, nh)][:],
                    start=(g == 0),
                    stop=(g == 1),
                )
            acc[(j, nh)] = a

        def add_x(j, nh):
            if nh == 0:
                y[j] = st3.tile([P, E], F32, name="y", tag="y")
                sums[j] = st5.tile([P, 2], F32, name="sums", tag="sums")
            cols = slice(NH * nh, NH * (nh + 1))
            nc.vector.scalar_tensor_tensor(
                out=y[j][:, cols], in0=acc[(j, nh)][:], scalar=1.0, in1=xs[j][:, cols],
                op0=ALU.mult, op1=ALU.add, accum_out=sums[j][:, nh:nh + 1],
            )

        def mean(j):
            nmean[j] = st5.tile([P, 1], F32, name="nmean", tag="nmean")
            nc.vector.tensor_scalar(
                out=nmean[j][:], in0=sums[j][:, 0:1], scalar1=sums[j][:, 1:2], scalar2=-1.0 / E,
                op0=ALU.add, op1=ALU.mult,
            )

        def stats(j):
            junk = st2.tile([P, E], F32, name="junk", tag="junk")
            ssq[j] = st5.tile([P, 1], F32, name="ssq", tag="ssq")
            nc.scalar.activation(
                out=junk[:], in_=y[j][:], func=ACT.Square, bias=nmean[j][:, 0:1], scale=1.0, accum_out=ssq[j][:],
            )

        def make_rstd(j):
            rstd[j] = st5.tile([P, 1], F32, name="rstd", tag="rstd")
            nc.scalar.activation(
                out=rstd[j][:], in_=ssq[j][:], func=ACT.Abs_reciprocal_sqrt, bias=LN_EPS, scale=1.0 / E
            )

        def centre_gamma(j):
            cen[j] = st3.tile([P, E], F32, name="cen", tag="cen")
            nc.vector.scalar_tensor_tensor(
                out=cen[j][:], in0=y[j][:], scalar=nmean[j][:, 0:1], in1=gam_ps[:], op0=ALU.add, op1=ALU.mult,
            )
            res[j] = st5.tile([P, E], F32, name="res", tag="res")
            res8[j] = st5.tile([P, E], FP8, name="res8", tag="res8")

        def scale_beta_v(j, c0, c1):
            nc.vector.scalar_tensor_tensor(
                out=res[j][:, c0:c1], in0=cen[j][:, c0:c1], scalar=rstd[j][:, 0:1], in1=bet_ps[:, c0:c1],
                op0=ALU.mult, op1=ALU.add,
            )

        def scale_beta_g(j, c0):
            w = st2.tile([P, E - CV], F32, name="w", tag="w")
            nc.gpsimd.tensor_scalar(
                out=w[:, c0 - CV:E - CV], in0=cen[j][:, c0:E], scalar1=rstd[j][:, 0:1], scalar2=0.0,
                op0=ALU.mult, op1=ALU.add,
            )
            nc.gpsimd.tensor_tensor(
                out=res[j][:, c0:E], in0=w[:, c0 - CV:E - CV], in1=beta_sb[:, c0 - CV:E - CV], op=ALU.add
            )

        def cast_s(j, c0, c1):
            nc.scalar.activation(
                out=res8[j][:, c0:c1], in_=res[j][:, c0:c1], func=ACT.Copy, scale=Y_SCALE, saturate=False
            )

        def cast_v(j, c0, c1):
            nc.vector.tensor_scalar(
                out=res8[j][:, c0:c1], in0=res[j][:, c0:c1], scalar1=Y_SCALE, scalar2=None, op0=ALU.mult,
                saturate=False,
            )

        def store0(j, c0, c1):
            nc.sync.dma_start(out=o0[j * P:(j + 1) * P, c0:c1], in_=res[j][:, c0:c1])

        def store1(j, c0, c1):
            nc.sync.dma_start(out=o1[j * P:(j + 1) * P, c0:c1], in_=res8[j][:, c0:c1].bitcast(U8))

        load_h(0)
        load_w(0, 0, 2)
        load_h(1)
        load_w(1, 0, 1)
        load_w(0, 1, 1)
        load_w(1, 1, 1)
        load_x(0)
        load_h(2)
        for j in range(1, PRELOAD):
            load_x(j)
            if j + 2 < PRELOAD:
                load_h(j + 2)

        gam_ps = ps_const.tile([P, E], BF16, name="gam_ps")
        bet_ps = ps_const.tile([P, E], BF16, name="bet_ps")

        def spread(dst, c0):
            for nh in range(2):
                nc.tensor.matmul(out=dst[:, NH * nh:NH * (nh + 1)], lhsT=ones[:],
                                 rhs=gbrow[:, c0 + NH * nh:c0 + NH * (nh + 1)], start=True, stop=True)

        def keep_clock(rhs):
            nc.tensor.matmul(out=bet_ps[:, 0:rhs.shape[1]], lhsT=ones[:], rhs=rhs, start=True, stop=True)

        for rep in range(16):
            keep_clock(ones[:])
        transposes(0)
        for c0 in (0, NH // 2):
            for t in range(2):
                keep_clock(wraw[(0, 0)][:, t, c0:c0 + NH // 2])
        w_copy_v(0, 0, 0, NH // 2)
        w_copy_v(0, 0, NH // 2, NH)
        copy_out(0)
        w_quant(0, 0)
        transposes(1)
        copy_out(1)
        quant(0)
        for t in range(2):
            keep_clock(wraw[(1, 0)][:, t, :])
        w_copy_v(1, 0, 0, W_SPLIT[(1, 0)])
        w_copy_s(1, 0)
        quant(1)
        for t in range(2):
            keep_clock(wraw[(0, 1)][:, t, :])
        w_quant(1, 0)
        matmuls(0, 0)
        w_copy_v(0, 1, 0, W_SPLIT[(0, 1)])
        w_copy_s(0, 1)
        for t in range(2):
            keep_clock(wraw[(1, 1)][:, t, :])
        w_copy_v(1, 1, 0, W_SPLIT[(1, 1)])
        w_copy_s(1, 1)
        w_quant(0, 1)
        spread(gam_ps, 0)
        spread(bet_ps, E)
        transposes(2)
        w_quant(1, 1)
        matmuls(0, 1)
        add_x(0, 0)
        nc.scalar.copy(out=beta_sb[:], in_=bet_ps[:, CV:E])
        matmuls(1, 0)
        matmuls(1, 1)
        add_x(0, 1)
        mean(0)
        copy_out(2)
        quant(2)
        stats(0)
        make_rstd(0)
        transposes(3)
        copy_out(3)

        for i in range(NT):
            if i + 2 < NT:
                matmuls(i + 2, 0)
            if i + 4 < NT:
                transposes(i + 4)
            if i + 2 < NT:
                matmuls(i + 2, 1)
            if i + 1 < NT:
                add_x(i + 1, 0)
                add_x(i + 1, 1)
            if 1 <= i < NT - 1:
                scale_beta_v(i - 1, 0, CV_TAIL.get(i - 1, CV))
            if i + 1 < NT:
                mean(i + 1)
                stats(i + 1)
            centre_gamma(i)
            if i == NT - 1:
                scale_beta_v(i - 1, 0, CV_TAIL.get(i - 1, CV))
            if i + 3 < NT:
                quant(i + 3)
            if i < NT - 1:
                scale_beta_g(i, CV_TAIL.get(i, CV))
            if i + 4 < NT:
                copy_out(i + 4)
            if i + 1 < NT:
                make_rstd(i + 1)
            if 1 <= i < NT - 1:
                store0(i - 1, 0, E)
                cast_s(i - 1, 0, E)
                store1(i - 1, 0, E)
                if i - 1 + PRELOAD < NT:
                    load_h(i - 1 + PRELOAD)
                    load_x(i - 1 + PRELOAD)

        last = NT - 1
        store0(last - 1, 0, E)
        cast_s(last - 1, 0, NH)
        store1(last - 1, 0, NH)
        scale_beta_v(last, 0, NH)
        store0(last, 0, NH)
        cast_s(last, 0, NH)
        store1(last, 0, NH)
        scale_beta_v(last, NH, E)
        store0(last, NH, E)
        cast_v(last - 1, NH, E)
        store1(last - 1, NH, E)
        cast_v(last, NH, E)
        store1(last, NH, E)
